import numpy as np
import ml_dtypes


def mxq(x, axis, fmt="e4m3"):
    dtype, down = {"e4m3": (ml_dtypes.float8_e4m3fn, 7), "e5m2": (ml_dtypes.float8_e5m2, 14)}[fmt]
    v = np.moveaxis(np.asarray(x, np.float32).astype(ml_dtypes.bfloat16).astype(np.float64), axis, -1)
    blocks = v.reshape(v.shape[:-1] + (-1, 32))
    amax = np.abs(blocks).max(-1, keepdims=True)
    byte = np.maximum(np.where(amax > 0, np.frexp(amax)[1] - 1 + 127, 0) - down, 1)
    scale = np.exp2(byte - 127.0)
    codes = (blocks / scale).astype(np.float32).astype(dtype).astype(np.float64)
    return np.moveaxis((codes * scale).reshape(v.shape), -1, axis)


WIDE = False


def mx_kscale(k):
    if not WIDE:
        return np.ones(k)
    levels = np.array([10, -10, 5, -5, 0])
    a = np.random.permutation(np.resize(levels, k // 512 * 4)).reshape(k // 512, 4)
    idx = np.arange(k)
    return np.exp2(a[idx // 512, idx % 128 // 32])


BF16 = ml_dtypes.bfloat16


def bf(x):
    return np.asarray(x, np.float32).astype(BF16)


def f64(x):
    return np.asarray(x).astype(np.float64)


B, HG, H, D, LSEQ, LK, BANK = 4, 48, 4, 128, 1536, 128, 128
N = HG * HG
C = H * D
DILATIONS = (1, 2, 3)
POOL = 2


def setup_inputs():
    s = mx_kscale(C)
    return {"x": bf(np.random.standard_normal((B, N, C)) * s),
            "W_kv": bf(np.random.standard_normal((C, 2 * C)) * 1.6 / np.sqrt(C) / s[:, None]),
            "b_kv": bf(np.random.standard_normal(2 * C) * 0.2),
            "E_k": bf(np.random.standard_normal((LSEQ, LK)) / np.sqrt(LSEQ)),
            "E_v": bf(np.random.standard_normal((LSEQ, LK)) / np.sqrt(LSEQ))}


def reference(x, W_kv, b_kv, E_k, E_v):
    xg = f64(x).reshape(B, HG, HG, C)
    x_multi = np.concatenate([xg[:, ::d, ::d, :].reshape(B, -1, C) for d in DILATIONS], axis=1)
    nm2 = (x_multi.shape[1] // POOL) * POOL
    x_pooled = x_multi[:, :nm2].reshape(B, nm2 // POOL, POOL, C).mean(axis=2)
    xl = x_pooled[:, :LSEQ]
    kv = (mxq(xl, 2, "e4m3") @ mxq(f64(W_kv), 0, "e4m3")) + f64(b_kv)
    k = kv[:, :, :C].reshape(B, LSEQ, H, D).transpose(0, 2, 1, 3)
    v = kv[:, :, C:].reshape(B, LSEQ, H, D).transpose(0, 2, 1, 3)
    k_comp = mxq(f64(E_k), 0, "e4m3").T @ mxq(k, 2, "e4m3")
    v_comp = mxq(f64(E_v), 0, "e4m3").T @ mxq(v, 2, "e4m3")
    return k_comp, v_comp

@@ -1,0 +1,284 @@
+from contextlib import ExitStack
+
+import concourse.mybir as mybir
+from concourse.masks import make_identity
+
+BF16 = mybir.dt.bfloat16
+F32 = mybir.dt.float32
+I32 = mybir.dt.int32
+U32 = mybir.dt.uint32
+U8 = mybir.dt.uint8
+FP8X4 = mybir.dt.float8_e4m3fn_x4
+ADD = mybir.AluOpType.add
+MULT = mybir.AluOpType.mult
+
+P = 128
+PACK = 4
+B = 4
+C = 512
+KV = 2 * C
+SLICES = KV // P
+J = 128
+HEADS = 4
+GROUPS = 3
+UNITS = B * GROUPS
+GROUP = P * PACK
+TOKENS = 2 * GROUP
+SLOTS = TOKENS // P
+LOAD_AHEAD = 5
+SCALAR_SLICES = 2
+
+FLOPS = 2 * B * GROUPS * GROUP * C * KV + 2 * B * 2 * J * GROUPS * GROUP * C
+
+
+def load_dense_tokens(nc, x_group, xg):
+    rows = x_group.rearrange("(a p) c -> p a c", p=P)
+    for m in range(PACK):
+        nc.sync.dma_start(out=xg[:, 2 * m : 2 * m + 2, :], in_=rows[:, 2 * m : 2 * m + 2, :])
+
+
+def load_tail_tokens(nc, x_b, xg):
+    nc.sync.dma_start(out=xg[0:32], in_=x_b[2048:2304, :].rearrange("(p i) c -> p i c", i=SLOTS))
+    step2 = x_b.rearrange("(r rr w i ii) c -> rr w ii r i c", rr=2, w=3, i=SLOTS, ii=2)
+    for w in range(3):
+        nc.sync.dma_start(out=xg[32 + w : 104 : 3], in_=step2[0, w, 0])
+    step3 = x_b.rearrange("(r rr w i ii) c -> rr w ii r i c", rr=3, w=2, i=SLOTS, ii=3)
+    for w in range(2):
+        nc.sync.dma_start(out=xg[104 + w : 128 : 2], in_=step3[0, w, 0, 0:12])
+
+
+def tile_efficientmultiscaledilatedattention_pa_t_kernel(tc, x, W_kv, b_kv, E_k, E_v, out_0, out_1):
+    nc = tc.nc
+    with ExitStack() as ctx:
+        const = ctx.enter_context(tc.tile_pool(name="const", bufs=1))
+        stream = ctx.enter_context(tc.tile_pool(name="stream", bufs=2))
+        psum = ctx.enter_context(tc.psum_pool(name="psum", bufs=1))
+        ctx.enter_context(tc.manual_schedule())
+
+        live = {}
+
+        def is_unit(u):
+            return 0 <= u < UNITS
+
+        def is_tail(u):
+            return u % GROUPS == GROUPS - 1
+
+        def load(u):
+            b, g = divmod(u, GROUPS)
+            xg = stream.tile([P, SLOTS, C], BF16, bufs=4)
+            if is_tail(u):
+                load_tail_tokens(nc, x[b], xg)
+            else:
+                load_dense_tokens(nc, x[b, g * TOKENS : (g + 1) * TOKENS, :], xg)
+            live["xg", u] = xg
+
+        def pool_tail(u):
+            pairs = live["xg", u][:].rearrange("p (m two) c -> p m two c", two=2)
+            xs = stream.tile([P, PACK, C], BF16)
+            nc.vector.tensor_tensor(
+                out=xs[:], in0=pairs[:, :, 0, :], in1=pairs[:, :, 1, :], op=ADD
+            )
+            live["xs", u] = xs
+
+        def sums(u):
+            xt = stream.tile([P, GROUP, PACK], BF16, align_bytes=64)
+            for m in range(PACK):
+                if is_tail(u):
+                    flipped = psum.tile([P, PACK, P], BF16, tag="xl", bufs=2)
+                    for t in range(PACK):
+                        nc.tensor.transpose(
+                            out=flipped[:, t, :],
+                            in_=live["xs", u][:, m, t * P : (t + 1) * P],
+                            identity=ident[:],
+                        )
+                else:
+                    flipped = psum.tile([P, PACK, P], F32, tag="xl", bufs=2)
+                    for a in range(2):
+                        for t in range(PACK):
+                            nc.tensor.matmul(
+                                out=flipped[:, t, a * 64 : (a + 1) * 64],
+                                lhsT=live["xg", u][:, 2 * m + a, t * P : (t + 1) * P],
+                                rhs=pair_sum[:],
+                                start=True,
+                                stop=True,
+                            )
+                nc.scalar.copy(
+                    out=xt[:, m * P : (m + 1) * P, :], in_=flipped[:].rearrange("q t c -> q c t")
+                )
+            live["xt", u] = xt
+
+        def quantise_x(u):
+            x_codes = stream.tile([P, GROUP], U32, align_bytes=64)
+            x_scales = stream.tile([P, GROUP], U8, align_bytes=64)
+            nc.vector.quantize_mx(
+                out=x_codes[:].bitcast(FP8X4),
+                scales=x_scales[:],
+                in_=live["xt", u][:].rearrange("q c t -> q (c t)"),
+            )
+            live["x_codes", u] = x_codes
+            live["x_scales", u] = x_scales
+
+        def products(u):
+            x_codes, x_scales = live["x_codes", u], live["x_scales", u]
+            kv = stream.tile([P, KV, PACK], BF16, align_bytes=64)
+            for cs in range(SLICES):
+                cols = slice(cs * P, (cs + 1) * P)
+                by_scalar = cs % 2 == 0 and cs // 2 < SCALAR_SLICES
+                if by_scalar:
+                    prod = psum.tile([P, PACK, P], F32, tag="prod_s", bufs=1)
+                else:
+                    prod = psum.tile([P, PACK, P], F32, tag="prod_v", bufs=3)
+                for m in range(PACK):
+                    nc.tensor.matmul_mx(
+                        out=prod[:, m, :],
+                        lhsT=x_codes[:, m * P : (m + 1) * P].bitcast(FP8X4),
+                        lhsT_scale=x_scales[:, m * P : (m + 1) * P],
+                        rhs=w_codes[:, cols].bitcast(FP8X4),
+                        rhs_scale=w_scales[:, cols],
+                        start=True,
+                        stop=True,
+                    )
+                bias_cols = bias[:, cols].unsqueeze(2).to_broadcast([P, P, PACK])
+                if by_scalar:
+                    halved = stream.tile([P, P, PACK], F32)
+                    nc.scalar.mul(out=halved[:], in_=prod[:].rearrange("p m c -> p c m"), mul=0.5)
+                    nc.gpsimd.tensor_tensor(
+                        out=kv[:, cols, :], in0=halved[:], in1=bias_cols, op=ADD
+                    )
+                else:
+                    nc.vector.scalar_tensor_tensor(
+                        out=kv[:, cols, :],
+                        in0=prod[:].rearrange("p m c -> p c m"),
+                        scalar=0.5,
+                        in1=bias_cols,
+                        op0=MULT,
+                        op1=ADD,
+                    )
+            live["kv", u] = kv
+
+        def quantise_kv(u):
+            kv_codes = stream.tile([P, KV], U32, align_bytes=64)
+            kv_scales = stream.tile([P, KV], U8, align_bytes=64)
+            for s in range(2):
+                cols = slice(s * C, (s + 1) * C)
+                nc.vector.quantize_mx(
+                    out=kv_codes[:, cols].bitcast(FP8X4),
+                    scales=kv_scales[:, cols],
+                    in_=live["kv", u][:, cols, :].rearrange("p c m -> p (c m)"),
+                )
+            live["kv_codes", u] = kv_codes
+            live["kv_scales", u] = kv_scales
+
+        def compress(u):
+            b, g = divmod(u, GROUPS)
+            if g == 0:
+                live["comp", b, 0] = psum.tile([J, C], F32, name="comp_k", tag="comp_k")
+                live["comp", b, 1] = psum.tile([J, C], F32, name="comp_v", tag="comp_v")
+            for s in range(2):
+                cols = slice(s * C, (s + 1) * C)
+                nc.tensor.matmul_mx(
+                    out=live["comp", b, s][:],
+                    lhsT=e_codes[:, g, s].bitcast(FP8X4),
+                    lhsT_scale=e_scales[:, g, s],
+                    rhs=live["kv_codes", u][:, cols].bitcast(FP8X4),
+                    rhs_scale=live["kv_scales", u][:, cols],
+                    start=(g == 0),
+                    stop=(g == GROUPS - 1),
+                )
+            if g == GROUPS - 1:
+                for s, out_dram in enumerate((out_0, out_1)):
+                    result = stream.tile([J, C], F32)
+                    nc.scalar.copy(out=result[:], in_=live["comp", b, s][:])
+                    nc.sync.dma_start(
+                        out=out_dram[b].rearrange("h j d -> j h d"),
+                        in_=result[:].rearrange("j (h d) -> j h d", h=HEADS),
+                    )
+
+        ident = const.tile([P, P], BF16)
+        make_identity(nc, ident[:])
+        bias_rows = const.tile([P, KV], BF16)
+        nc.vector.memset(bias_rows[:].bitcast(I32), 0)
+        nc.scalar.dma_start(out=bias_rows[0:1, :], in_=b_kv.rearrange("(o c) -> o c", o=1))
+        ones = const.tile([P, P], BF16)
+        nc.vector.memset(ones[:], 1.0)
+
+        w_raw = const.tile([P, PACK, KV], BF16)
+        w_rows = W_kv.rearrange("(t q) c -> q t c", t=PACK)
+        for half in range(2):
+            cols = slice(half * C, (half + 1) * C)
+            nc.sync.dma_start(out=w_raw[:, :, cols], in_=w_rows[:, :, cols])
+        load(0)
+        load(1)
+        e_raw = const.tile([P, GROUPS, 2, PACK, J], BF16)
+        for g in range(GROUPS):
+            order = "(p m) j -> p m j" if is_tail(g) else "(m p) j -> p m j"
+            for s, e_dram in enumerate((E_k, E_v)):
+                nc.sync.dma_start(
+                    out=e_raw[:, g, s],
+                    in_=e_dram[g * GROUP : (g + 1) * GROUP, :].rearrange(order, m=PACK),
+                )
+        load(2)
+
+        pair_sum = const.tile([P, P // 2], BF16)
+        ident_pairs = ident[:].rearrange("p (l two) -> p l two", two=2)
+        nc.vector.tensor_tensor(
+            out=pair_sum[:], in0=ident_pairs[:, :, 0], in1=ident_pairs[:, :, 1], op=ADD
+        )
+        bias = const.tile([P, KV], BF16)
+        for half in range(2):
+            cols = slice(half * C, (half + 1) * C)
+            spread = psum.tile([P, C], F32, tag="prod_v", bufs=3)
+            nc.tensor.matmul(
+                out=spread[:], lhsT=ones[:], rhs=bias_rows[:, cols], start=True, stop=True
+            )
+            nc.scalar.copy(out=bias[:, cols], in_=spread[:])
+
+        w_grouped = const.tile([P, KV, PACK], BF16, align_bytes=64)
+        w_codes = const.tile([P, KV], U32, align_bytes=64)
+        w_scales = const.tile([P, KV], U8, align_bytes=64)
+        for half in range(2):
+            cols = slice(half * C, (half + 1) * C)
+            nc.vector.tensor_copy(
+                out=w_grouped[:, cols, :], in_=w_raw[:, :, cols].rearrange("q t c -> q c t")
+            )
+        for half in range(2):
+            cols = slice(half * C, (half + 1) * C)
+            nc.vector.quantize_mx(
+                out=w_codes[:, cols].bitcast(FP8X4),
+                scales=w_scales[:, cols],
+                in_=w_grouped[:, cols, :].rearrange("q c t -> q (c t)"),
+            )
+
+        e_grouped = const.tile([P, GROUPS, 2, J, PACK], BF16, align_bytes=64)
+        e_codes = const.tile([P, GROUPS, 2, J], U32, align_bytes=64)
+        e_scales = const.tile([P, GROUPS, 2, J], U8, align_bytes=64)
+
+        def regroup_e(g):
+            nc.scalar.copy(out=e_grouped[:, g], in_=e_raw[:, g].rearrange("p s m j -> p s j m"))
+
+        def quantise_e(g):
+            nc.vector.quantize_mx(
+                out=e_codes[:, g].rearrange("p s j -> p (s j)").bitcast(FP8X4),
+                scales=e_scales[:, g].rearrange("p s j -> p (s j)"),
+                in_=e_grouped[:, g].rearrange("p s j m -> p (s j m)"),
+            )
+
+        for i in range(-2, UNITS + 1):
+            if is_unit(i + LOAD_AHEAD) and i + LOAD_AHEAD > 2:
+                load(i + LOAD_AHEAD)
+            if is_unit(i):
+                products(i)
+            if is_unit(i + 2) and is_tail(i + 2):
+                pool_tail(i + 2)
+            if is_unit(i - 1):
+                compress(i - 1)
+            if is_unit(i + 2):
+                sums(i + 2)
+            if 0 <= i + 1 < GROUPS:
+                regroup_e(i + 1)
+            if 0 <= i < GROUPS:
+                quantise_e(i)
+            if is_unit(i + 1):
+                quantise_x(i + 1)
+            if is_unit(i):
+                quantise_kv(i)

@@ -26,7 +26,7 @@ GROUP = P * PACK
 TOKENS = 2 * GROUP
 SLOTS = TOKENS // P
 LOAD_AHEAD = 5
-SCALAR_SLICES = 2
+SCALAR_SLICES = 3
 
 FLOPS = 2 * B * GROUPS * GROUP * C * KV + 2 * B * 2 * J * GROUPS * GROUP * C
 
@@ -80,32 +80,32 @@ def tile_efficientmultiscaledilatedattention_pa_t_kernel(tc, x, W_kv, b_kv, E_k,
             )
             live["xs", u] = xs
 
-        def sums(u):
-            xt = stream.tile([P, GROUP, PACK], BF16, align_bytes=64)
-            for m in range(PACK):
-                if is_tail(u):
-                    flipped = psum.tile([P, PACK, P], BF16, tag="xl", bufs=2)
+        def sums_tile(u, m):
+            if m == 0:
+                live["xt", u] = stream.tile([P, GROUP, PACK], BF16, name="xt", align_bytes=64)
+            if is_tail(u):
+                flipped = psum.tile([P, PACK, P], BF16, tag="xl", bufs=2)
+                for t in range(PACK):
+                    nc.tensor.transpose(
+                        out=flipped[:, t, :],
+                        in_=live["xs", u][:, m, t * P : (t + 1) * P],
+                        identity=ident[:],
+                    )
+            else:
+                flipped = psum.tile([P, PACK, P], F32, tag="xl", bufs=2)
+                for a in range(2):
                     for t in range(PACK):
-                        nc.tensor.transpose(
-                            out=flipped[:, t, :],
-                            in_=live["xs", u][:, m, t * P : (t + 1) * P],
-                            identity=ident[:],
+                        nc.tensor.matmul(
+                            out=flipped[:, t, a * 64 : (a + 1) * 64],
+                            lhsT=live["xg", u][:, 2 * m + a, t * P : (t + 1) * P],
+                            rhs=pair_sum[:],
+                            start=True,
+                            stop=True,
                         )
-                else:
-                    flipped = psum.tile([P, PACK, P], F32, tag="xl", bufs=2)
-                    for a in range(2):
-                        for t in range(PACK):
-                            nc.tensor.matmul(
-                                out=flipped[:, t, a * 64 : (a + 1) * 64],
-                                lhsT=live["xg", u][:, 2 * m + a, t * P : (t + 1) * P],
-                                rhs=pair_sum[:],
-                                start=True,
-                                stop=True,
-                            )
-                nc.scalar.copy(
-                    out=xt[:, m * P : (m + 1) * P, :], in_=flipped[:].rearrange("q t c -> q c t")
-                )
-            live["xt", u] = xt
+            nc.scalar.copy(
+                out=live["xt", u][:, m * P : (m + 1) * P, :],
+                in_=flipped[:].rearrange("q t c -> q c t"),
+            )
 
         def quantise_x(u):
             x_codes = stream.tile([P, GROUP], U32, align_bytes=64)
@@ -118,47 +118,44 @@ def tile_efficientmultiscaledilatedattention_pa_t_kernel(tc, x, W_kv, b_kv, E_k,
             live["x_codes", u] = x_codes
             live["x_scales", u] = x_scales
 
-        def products(u):
-            x_codes, x_scales = live["x_codes", u], live["x_scales", u]
-            kv = stream.tile([P, KV, PACK], BF16, align_bytes=64)
-            for cs in range(SLICES):
-                cols = slice(cs * P, (cs + 1) * P)
-                by_scalar = cs % 2 == 0 and cs // 2 < SCALAR_SLICES
-                if by_scalar:
-                    prod = psum.tile([P, PACK, P], F32, tag="prod_s", bufs=1)
-                else:
-                    prod = psum.tile([P, PACK, P], F32, tag="prod_v", bufs=3)
-                for m in range(PACK):
-                    nc.tensor.matmul_mx(
-                        out=prod[:, m, :],
-                        lhsT=x_codes[:, m * P : (m + 1) * P].bitcast(FP8X4),
-                        lhsT_scale=x_scales[:, m * P : (m + 1) * P],
-                        rhs=w_codes[:, cols].bitcast(FP8X4),
-                        rhs_scale=w_scales[:, cols],
-                        start=True,
-                        stop=True,
-                    )
-                bias_cols = bias[:, cols].unsqueeze(2).to_broadcast([P, P, PACK])
-                if by_scalar:
-                    halved = stream.tile([P, P, PACK], F32)
-                    nc.scalar.mul(out=halved[:], in_=prod[:].rearrange("p m c -> p c m"), mul=0.5)
-                    nc.gpsimd.tensor_tensor(
-                        out=kv[:, cols, :], in0=halved[:], in1=bias_cols, op=ADD
-                    )
-                else:
-                    nc.vector.scalar_tensor_tensor(
-                        out=kv[:, cols, :],
-                        in0=prod[:].rearrange("p m c -> p c m"),
-                        scalar=0.5,
-                        in1=bias_cols,
-                        op0=MULT,
-                        op1=ADD,
-                    )
-            live["kv", u] = kv
+        def product(u, cs):
+            if cs == 0:
+                live["kv", u] = stream.tile([P, KV, PACK], BF16, name="kv", align_bytes=64)
+            x_codes, x_scales, kv = live["x_codes", u], live["x_scales", u], live["kv", u]
+            cols = slice(cs * P, (cs + 1) * P)
+            by_scalar = cs % 2 == 0 and cs // 2 < SCALAR_SLICES
+            if by_scalar:
+                prod = psum.tile([P, PACK, P], F32, tag="prod_s", bufs=2)
+            else:
+                prod = psum.tile([P, PACK, P], F32, tag="prod_v", bufs=4)
+            for m in range(PACK):
+                nc.tensor.matmul_mx(
+                    out=prod[:, m, :],
+                    lhsT=x_codes[:, m * P : (m + 1) * P].bitcast(FP8X4),
+                    lhsT_scale=x_scales[:, m * P : (m + 1) * P],
+                    rhs=w_codes[:, cols].bitcast(FP8X4),
+                    rhs_scale=w_scales[:, cols],
+                    start=True,
+                    stop=True,
+                )
+            bias_cols = bias[:, cols].unsqueeze(2).to_broadcast([P, P, PACK])
+            if by_scalar:
+                halved = stream.tile([P, P, PACK], F32, bufs=3)
+                nc.scalar.mul(out=halved[:], in_=prod[:].rearrange("p m c -> p c m"), mul=0.5)
+                nc.gpsimd.tensor_tensor(out=kv[:, cols, :], in0=halved[:], in1=bias_cols, op=ADD)
+            else:
+                nc.vector.scalar_tensor_tensor(
+                    out=kv[:, cols, :],
+                    in0=prod[:].rearrange("p m c -> p c m"),
+                    scalar=0.5,
+                    in1=bias_cols,
+                    op0=MULT,
+                    op1=ADD,
+                )
 
         def quantise_kv(u):
-            kv_codes = stream.tile([P, KV], U32, align_bytes=64)
-            kv_scales = stream.tile([P, KV], U8, align_bytes=64)
+            kv_codes = stream.tile([P, KV], U32, bufs=4, align_bytes=64)
+            kv_scales = stream.tile([P, KV], U8, bufs=4, align_bytes=64)
             for s in range(2):
                 cols = slice(s * C, (s + 1) * C)
                 nc.vector.quantize_mx(
@@ -169,30 +166,31 @@ def tile_efficientmultiscaledilatedattention_pa_t_kernel(tc, x, W_kv, b_kv, E_k,
             live["kv_codes", u] = kv_codes
             live["kv_scales", u] = kv_scales
 
-        def compress(u):
-            b, g = divmod(u, GROUPS)
-            if g == 0:
-                live["comp", b, 0] = psum.tile([J, C], F32, name="comp_k", tag="comp_k")
-                live["comp", b, 1] = psum.tile([J, C], F32, name="comp_v", tag="comp_v")
-            for s in range(2):
-                cols = slice(s * C, (s + 1) * C)
-                nc.tensor.matmul_mx(
-                    out=live["comp", b, s][:],
-                    lhsT=e_codes[:, g, s].bitcast(FP8X4),
-                    lhsT_scale=e_scales[:, g, s],
-                    rhs=live["kv_codes", u][:, cols].bitcast(FP8X4),
-                    rhs_scale=live["kv_scales", u][:, cols],
-                    start=(g == 0),
-                    stop=(g == GROUPS - 1),
-                )
-            if g == GROUPS - 1:
-                for s, out_dram in enumerate((out_0, out_1)):
-                    result = stream.tile([J, C], F32)
-                    nc.scalar.copy(out=result[:], in_=live["comp", b, s][:])
-                    nc.sync.dma_start(
-                        out=out_dram[b].rearrange("h j d -> j h d"),
-                        in_=result[:].rearrange("j (h d) -> j h d", h=HEADS),
+        def compress(b):
+            comp = [
+                psum.tile([J, C], F32, name="comp_k", tag="prod_v", bufs=4),
+                psum.tile([J, C], F32, name="comp_v", tag="prod_v", bufs=4),
+            ]
+            for g in range(GROUPS):
+                u = b * GROUPS + g
+                for s in range(2):
+                    cols = slice(s * C, (s + 1) * C)
+                    nc.tensor.matmul_mx(
+                        out=comp[s][:],
+                        lhsT=e_codes[:, g, s].bitcast(FP8X4),
+                        lhsT_scale=e_scales[:, g, s],
+                        rhs=live["kv_codes", u][:, cols].bitcast(FP8X4),
+                        rhs_scale=live["kv_scales", u][:, cols],
+                        start=(g == 0),
+                        stop=(g == GROUPS - 1),
                     )
+            for s, out_dram in enumerate((out_0, out_1)):
+                result = stream.tile([J, C], F32)
+                nc.scalar.copy(out=result[:], in_=comp[s][:])
+                nc.sync.dma_start(
+                    out=out_dram[b].rearrange("h j d -> j h d"),
+                    in_=result[:].rearrange("j (h d) -> j h d", h=HEADS),
+                )
 
         ident = const.tile([P, P], BF16)
         make_identity(nc, ident[:])
@@ -209,6 +207,7 @@ def tile_efficientmultiscaledilatedattention_pa_t_kernel(tc, x, W_kv, b_kv, E_k,
             nc.sync.dma_start(out=w_raw[:, :, cols], in_=w_rows[:, :, cols])
         load(0)
         load(1)
+        load(2)
         e_raw = const.tile([P, GROUPS, 2, PACK, J], BF16)
         for g in range(GROUPS):
             order = "(p m) j -> p m j" if is_tail(g) else "(m p) j -> p m j"
@@ -217,7 +216,6 @@ def tile_efficientmultiscaledilatedattention_pa_t_kernel(tc, x, W_kv, b_kv, E_k,
                     out=e_raw[:, g, s],
                     in_=e_dram[g * GROUP : (g + 1) * GROUP, :].rearrange(order, m=PACK),
                 )
-        load(2)
 
         pair_sum = const.tile([P, P // 2], BF16)
         ident_pairs = ident[:].rearrange("p (l two) -> p l two", two=2)
@@ -227,7 +225,7 @@ def tile_efficientmultiscaledilatedattention_pa_t_kernel(tc, x, W_kv, b_kv, E_k,
         bias = const.tile([P, KV], BF16)
         for half in range(2):
             cols = slice(half * C, (half + 1) * C)
-            spread = psum.tile([P, C], F32, tag="prod_v", bufs=3)
+            spread = psum.tile([P, C], F32, tag="prod_v", bufs=4)
             nc.tensor.matmul(
                 out=spread[:], lhsT=ones[:], rhs=bias_rows[:, cols], start=True, stop=True
             )
@@ -263,22 +261,23 @@ def tile_efficientmultiscaledilatedattention_pa_t_kernel(tc, x, W_kv, b_kv, E_k,
                 in_=e_grouped[:, g].rearrange("p s j m -> p (s j m)"),
             )
 
-        for i in range(-2, UNITS + 1):
+        for i in range(-2, UNITS + 2):
             if is_unit(i + LOAD_AHEAD) and i + LOAD_AHEAD > 2:
                 load(i + LOAD_AHEAD)
-            if is_unit(i):
-                products(i)
-            if is_unit(i + 2) and is_tail(i + 2):
-                pool_tail(i + 2)
-            if is_unit(i - 1):
-                compress(i - 1)
-            if is_unit(i + 2):
-                sums(i + 2)
-            if 0 <= i + 1 < GROUPS:
-                regroup_e(i + 1)
-            if 0 <= i < GROUPS:
-                quantise_e(i)
+            if 0 <= i - 1 < GROUPS:
+                quantise_e(i - 1)
             if is_unit(i + 1):
                 quantise_x(i + 1)
-            if is_unit(i):
-                quantise_kv(i)
+            if is_unit(i - 1):
+                quantise_kv(i - 1)
+            for cs in range(SLICES):
+                if is_unit(i):
+                    product(i, cs)
+                if cs % 2 == 1 and is_unit(i + 2):
+                    sums_tile(i + 2, cs // 2)
+                if cs == SLICES // 2 - 1 and is_unit(i - 2) and is_tail(i - 2):
+                    compress((i - 2) // GROUPS)
+            if is_unit(i + 3) and is_tail(i + 3):
+                pool_tail(i + 3)
+            if 0 <= i < GROUPS:
+                regroup_e(i)

@@ -26,7 +26,7 @@ GROUP = P * PACK
 TOKENS = 2 * GROUP
 SLOTS = TOKENS // P
 LOAD_AHEAD = 5
-SCALAR_SLICES = 3
+SCALAR_SLICES = 2
 
 FLOPS = 2 * B * GROUPS * GROUP * C * KV + 2 * B * 2 * J * GROUPS * GROUP * C
 

@@ -83,29 +83,33 @@ def tile_efficientmultiscaledilatedattention_pa_t_kernel(tc, x, W_kv, b_kv, E_k,
         def sums_tile(u, m):
             if m == 0:
                 live["xt", u] = stream.tile([P, GROUP, PACK], BF16, name="xt", align_bytes=64)
+            if m % 2 == 0:
+                live["flipped", u] = psum.tile([P, 2, PACK, P], BF16, name="flipped", tag="xl", bufs=2)
+            flipped = live["flipped", u]
             if is_tail(u):
-                flipped = psum.tile([P, PACK, P], BF16, tag="xl", bufs=2)
                 for t in range(PACK):
                     nc.tensor.transpose(
-                        out=flipped[:, t, :],
+                        out=flipped[:, m % 2, t, :],
                         in_=live["xs", u][:, m, t * P : (t + 1) * P],
                         identity=ident[:],
                     )
             else:
-                flipped = psum.tile([P, PACK, P], F32, tag="xl", bufs=2)
                 for a in range(2):
                     for t in range(PACK):
                         nc.tensor.matmul(
-                            out=flipped[:, t, a * 64 : (a + 1) * 64],
+                            out=flipped[:, m % 2, t, a * 64 : (a + 1) * 64],
                             lhsT=live["xg", u][:, 2 * m + a, t * P : (t + 1) * P],
                             rhs=pair_sum[:],
                             start=True,
                             stop=True,
                         )
-            nc.scalar.copy(
-                out=live["xt", u][:, m * P : (m + 1) * P, :],
-                in_=flipped[:].rearrange("q t c -> q c t"),
-            )
+            if m % 2 == 1:
+                nc.scalar.copy(
+                    out=live["xt", u][:, (m - 1) * P : (m + 1) * P, :].rearrange(
+                        "q (k c) t -> q k c t", k=2
+                    ),
+                    in_=flipped[:].rearrange("q k t c -> q k c t"),
+                )
 
         def quantise_x(u):
             x_codes = stream.tile([P, GROUP], U32, align_bytes=64)

@@ -11,6 +11,7 @@ U8 = mybir.dt.uint8
 FP8X4 = mybir.dt.float8_e4m3fn_x4
 ADD = mybir.AluOpType.add
 MULT = mybir.AluOpType.mult
+IDENTITY = mybir.ActivationFunctionType.Identity
 
 P = 128
 PACK = 4
@@ -26,7 +27,8 @@ GROUP = P * PACK
 TOKENS = 2 * GROUP
 SLOTS = TOKENS // P
 LOAD_AHEAD = 5
-SCALAR_SLICES = 2
+HALF = SLICES // 2
+TURNED = 2
 
 FLOPS = 2 * B * GROUPS * GROUP * C * KV + 2 * B * 2 * J * GROUPS * GROUP * C
 
@@ -80,6 +82,10 @@ def tile_efficientmultiscaledilatedattention_pa_t_kernel(tc, x, W_kv, b_kv, E_k,
             )
             live["xs", u] = xs
 
+        def sums(u, half):
+            for m in (2 * half, 2 * half + 1):
+                sums_tile(u, m)
+
         def sums_tile(u, m):
             if m == 0:
                 live["xt", u] = stream.tile([P, GROUP, PACK], BF16, name="xt", align_bytes=64)
@@ -122,16 +128,13 @@ def tile_efficientmultiscaledilatedattention_pa_t_kernel(tc, x, W_kv, b_kv, E_k,
             live["x_codes", u] = x_codes
             live["x_scales", u] = x_scales
 
-        def product(u, cs):
-            if cs == 0:
-                live["kv", u] = stream.tile([P, KV, PACK], BF16, name="kv", align_bytes=64)
-            x_codes, x_scales, kv = live["x_codes", u], live["x_scales", u], live["kv", u]
+        def new_kv(u):
+            live["kv", u] = stream.tile([P, KV, PACK], BF16, name="kv", align_bytes=64)
+
+        def direct(u, cs):
+            x_codes, x_scales = live["x_codes", u], live["x_scales", u]
             cols = slice(cs * P, (cs + 1) * P)
-            by_scalar = cs % 2 == 0 and cs // 2 < SCALAR_SLICES
-            if by_scalar:
-                prod = psum.tile([P, PACK, P], F32, tag="prod_s", bufs=2)
-            else:
-                prod = psum.tile([P, PACK, P], F32, tag="prod_v", bufs=4)
+            prod = psum.tile([P, PACK, P], F32, tag="prod_v", bufs=3)
             for m in range(PACK):
                 nc.tensor.matmul_mx(
                     out=prod[:, m, :],
@@ -142,38 +145,70 @@ def tile_efficientmultiscaledilatedattention_pa_t_kernel(tc, x, W_kv, b_kv, E_k,
                     start=True,
                     stop=True,
                 )
-            bias_cols = bias[:, cols].unsqueeze(2).to_broadcast([P, P, PACK])
-            if by_scalar:
-                halved = stream.tile([P, P, PACK], F32, bufs=3)
-                nc.scalar.mul(out=halved[:], in_=prod[:].rearrange("p m c -> p c m"), mul=0.5)
-                nc.gpsimd.tensor_tensor(out=kv[:, cols, :], in0=halved[:], in1=bias_cols, op=ADD)
-            else:
-                nc.vector.scalar_tensor_tensor(
-                    out=kv[:, cols, :],
-                    in0=prod[:].rearrange("p m c -> p c m"),
-                    scalar=0.5,
-                    in1=bias_cols,
-                    op0=MULT,
-                    op1=ADD,
-                )
+            nc.vector.scalar_tensor_tensor(
+                out=live["kv", u][:, cols, :],
+                in0=prod[:].rearrange("p m c -> p c m"),
+                scalar=0.5,
+                in1=bias[:, cols].unsqueeze(2).to_broadcast([P, P, PACK]),
+                op0=MULT,
+                op1=ADD,
+            )
 
-        def quantise_kv(u):
-            kv_codes = stream.tile([P, KV], U32, bufs=4, align_bytes=64)
-            kv_scales = stream.tile([P, KV], U8, bufs=4, align_bytes=64)
-            for s in range(2):
-                cols = slice(s * C, (s + 1) * C)
-                nc.vector.quantize_mx(
-                    out=kv_codes[:, cols].bitcast(FP8X4),
-                    scales=kv_scales[:, cols],
-                    in_=live["kv", u][:, cols, :].rearrange("p c m -> p (c m)"),
+        def turned(u, half):
+            x_codes, x_scales = live["x_codes", u], live["x_scales", u]
+            flat = stream.tile([P, TURNED, 2, P, 2], BF16, name="flat", align_bytes=64, bufs=3)
+            for n in range(TURNED):
+                cs = half * HALF + n
+                cols = slice(cs * P, (cs + 1) * P)
+                prod = psum.tile([P, GROUP], F32, tag="prod_s", bufs=2)
+                nc.tensor.matmul_mx(
+                    out=prod[:],
+                    lhsT=w_codes[:, cols].bitcast(FP8X4),
+                    lhsT_scale=w_scales[:, cols],
+                    rhs=x_codes[:].bitcast(FP8X4),
+                    rhs_scale=x_scales[:],
+                    start=True,
+                    stop=True,
                 )
-            live["kv_codes", u] = kv_codes
-            live["kv_scales", u] = kv_scales
+                nc.scalar.activation(
+                    out=flat[:, n],
+                    in_=prod[:].rearrange("c (h e p) -> c h p e", h=2, e=2),
+                    func=IDENTITY,
+                    bias=bias_cols[:, cs : cs + 1],
+                    scale=0.5,
+                )
+            live["flat", u, half] = flat
+
+        def turn(u, half):
+            words = live["flat", u, half][:].rearrange("c n h p e -> c (n h) (p e)").bitcast(F32)
+            bank = psum.tile([P, TURNED, 2, P], F32, tag="turned", bufs=1)
+            for n in range(TURNED):
+                for h in range(2):
+                    nc.tensor.transpose(
+                        out=bank[:, n, h, :], in_=words[:, 2 * n + h, :], identity=ident_words[:]
+                    )
+            cols = slice(half * C, half * C + TURNED * P)
+            kv_words = live["kv", u][:, cols, :].rearrange("p c m -> p (c m)").bitcast(F32)
+            nc.scalar.copy(
+                out=kv_words.rearrange("p (n c h) -> p n c h", n=TURNED, h=2),
+                in_=bank[:].rearrange("p n h c -> p n c h"),
+            )
+
+        def quantise_kv(u, half):
+            if half == 0:
+                live["kv_codes", u] = stream.tile([P, KV], U32, name="kv_codes", bufs=4, align_bytes=64)
+                live["kv_scales", u] = stream.tile([P, KV], U8, name="kv_scales", bufs=4, align_bytes=64)
+            cols = slice(half * C, (half + 1) * C)
+            nc.vector.quantize_mx(
+                out=live["kv_codes", u][:, cols].bitcast(FP8X4),
+                scales=live["kv_scales", u][:, cols],
+                in_=live["kv", u][:, cols, :].rearrange("p c m -> p (c m)"),
+            )
 
         def compress(b):
             comp = [
-                psum.tile([J, C], F32, name="comp_k", tag="prod_v", bufs=4),
-                psum.tile([J, C], F32, name="comp_v", tag="prod_v", bufs=4),
+                psum.tile([J, C], F32, name="comp_k", tag="prod_v", bufs=3),
+                psum.tile([J, C], F32, name="comp_v", tag="prod_v", bufs=3),
             ]
             for g in range(GROUPS):
                 u = b * GROUPS + g
@@ -198,6 +233,8 @@ def tile_efficientmultiscaledilatedattention_pa_t_kernel(tc, x, W_kv, b_kv, E_k,
 
         ident = const.tile([P, P], BF16)
         make_identity(nc, ident[:])
+        ident_words = const.tile([P, P], F32)
+        make_identity(nc, ident_words[:])
         bias_rows = const.tile([P, KV], BF16)
         nc.vector.memset(bias_rows[:].bitcast(I32), 0)
         nc.scalar.dma_start(out=bias_rows[0:1, :], in_=b_kv.rearrange("(o c) -> o c", o=1))
@@ -229,11 +266,22 @@ def tile_efficientmultiscaledilatedattention_pa_t_kernel(tc, x, W_kv, b_kv, E_k,
         bias = const.tile([P, KV], BF16)
         for half in range(2):
             cols = slice(half * C, (half + 1) * C)
-            spread = psum.tile([P, C], F32, tag="prod_v", bufs=4)
+            spread = psum.tile([P, C], F32, tag="prod_v", bufs=3)
             nc.tensor.matmul(
                 out=spread[:], lhsT=ones[:], rhs=bias_rows[:, cols], start=True, stop=True
             )
             nc.scalar.copy(out=bias[:, cols], in_=spread[:])
+        upright = psum.tile([P, SLICES], F32, tag="prod_v", bufs=3)
+        for cs in range(SLICES):
+            nc.tensor.matmul(
+                out=upright[:, cs : cs + 1],
+                lhsT=bias_rows[:, cs * P : (cs + 1) * P],
+                rhs=ones[:, 0:1],
+                start=True,
+                stop=True,
+            )
+        bias_cols = const.tile([P, SLICES], F32)
+        nc.scalar.copy(out=bias_cols[:], in_=upright[:])
 
         w_grouped = const.tile([P, KV, PACK], BF16, align_bytes=64)
         w_codes = const.tile([P, KV], U32, align_bytes=64)
@@ -266,21 +314,36 @@ def tile_efficientmultiscaledilatedattention_pa_t_kernel(tc, x, W_kv, b_kv, E_k,
             )
 
         for i in range(-2, UNITS + 2):
+            now, before, ahead = is_unit(i), is_unit(i - 1), is_unit(i + 2)
             if is_unit(i + LOAD_AHEAD) and i + LOAD_AHEAD > 2:
                 load(i + LOAD_AHEAD)
             if 0 <= i - 1 < GROUPS:
                 quantise_e(i - 1)
             if is_unit(i + 1):
                 quantise_x(i + 1)
-            if is_unit(i - 1):
-                quantise_kv(i - 1)
-            for cs in range(SLICES):
-                if is_unit(i):
-                    product(i, cs)
-                if cs % 2 == 1 and is_unit(i + 2):
-                    sums_tile(i + 2, cs // 2)
-                if cs == SLICES // 2 - 1 and is_unit(i - 2) and is_tail(i - 2):
-                    compress((i - 2) // GROUPS)
+            if now:
+                new_kv(i)
+                turned(i, 0)
+                direct(i, 2)
+            if before:
+                turn(i - 1, 1)
+            if ahead:
+                sums(i + 2, 0)
+            if now:
+                direct(i, 3)
+                turned(i, 1)
+            if before:
+                quantise_kv(i - 1, 1)
+            if now:
+                turn(i, 0)
+            if ahead:
+                sums(i + 2, 1)
+            if now:
+                direct(i, 6)
+                direct(i, 7)
+                quantise_kv(i, 0)
+            if before and is_tail(i - 1):
+                compress((i - 1) // GROUPS)
             if is_unit(i + 3) and is_tail(i + 3):
                 pool_tail(i + 3)
             if 0 <= i < GROUPS:

@@ -27,6 +27,7 @@ GROUP = P * PACK
 TOKENS = 2 * GROUP
 SLOTS = TOKENS // P
 LOAD_AHEAD = 5
+FIRST_LOADS = 4
 HALF = SLICES // 2
 TURNED = 2
 
@@ -34,9 +35,10 @@ FLOPS = 2 * B * GROUPS * GROUP * C * KV + 2 * B * 2 * J * GROUPS * GROUP * C
 
 
 def load_dense_tokens(nc, x_group, xg):
-    rows = x_group.rearrange("(a p) c -> p a c", p=P)
-    for m in range(PACK):
-        nc.sync.dma_start(out=xg[:, 2 * m : 2 * m + 2, :], in_=rows[:, 2 * m : 2 * m + 2, :])
+    rows = x_group.rearrange("(p i) c -> p i c", i=SLOTS)
+    for half in range(2):
+        part = slice(half * SLOTS // 2, (half + 1) * SLOTS // 2)
+        nc.sync.dma_start(out=xg[:, part, :], in_=rows[:, part, :])
 
 
 def load_tail_tokens(nc, x_b, xg):
@@ -74,48 +76,34 @@ def tile_efficientmultiscaledilatedattention_pa_t_kernel(tc, x, W_kv, b_kv, E_k,
                 load_dense_tokens(nc, x[b, g * TOKENS : (g + 1) * TOKENS, :], xg)
             live["xg", u] = xg
 
-        def pool_tail(u):
+        def pool(u, half):
+            if half == 0:
+                live["xs", u] = stream.tile([P, PACK, C], BF16, name="xs")
             pairs = live["xg", u][:].rearrange("p (m two) c -> p m two c", two=2)
-            xs = stream.tile([P, PACK, C], BF16)
+            two_m = slice(2 * half, 2 * half + 2)
             nc.vector.tensor_tensor(
-                out=xs[:], in0=pairs[:, :, 0, :], in1=pairs[:, :, 1, :], op=ADD
+                out=live["xs", u][:, two_m, :],
+                in0=pairs[:, two_m, 0, :],
+                in1=pairs[:, two_m, 1, :],
+                op=ADD,
             )
-            live["xs", u] = xs
 
         def sums(u, half):
-            for m in (2 * half, 2 * half + 1):
-                sums_tile(u, m)
-
-        def sums_tile(u, m):
-            if m == 0:
+            if half == 0:
                 live["xt", u] = stream.tile([P, GROUP, PACK], BF16, name="xt", align_bytes=64)
-            if m % 2 == 0:
-                live["flipped", u] = psum.tile([P, 2, PACK, P], BF16, name="flipped", tag="xl", bufs=2)
-            flipped = live["flipped", u]
-            if is_tail(u):
-                for t in range(PACK):
+            bank = psum.tile([P, 2, 2, P], F32, tag="xl", bufs=2)
+            words = live["xs", u][:].rearrange("p m c -> p (m c)").bitcast(F32)
+            for k in range(2):
+                for h in range(2):
+                    start = ((2 * half + k) * 2 + h) * P
                     nc.tensor.transpose(
-                        out=flipped[:, m % 2, t, :],
-                        in_=live["xs", u][:, m, t * P : (t + 1) * P],
-                        identity=ident[:],
+                        out=bank[:, k, h, :], in_=words[:, start : start + P], identity=ident_words[:]
                     )
-            else:
-                for a in range(2):
-                    for t in range(PACK):
-                        nc.tensor.matmul(
-                            out=flipped[:, m % 2, t, a * 64 : (a + 1) * 64],
-                            lhsT=live["xg", u][:, 2 * m + a, t * P : (t + 1) * P],
-                            rhs=pair_sum[:],
-                            start=True,
-                            stop=True,
-                        )
-            if m % 2 == 1:
-                nc.scalar.copy(
-                    out=live["xt", u][:, (m - 1) * P : (m + 1) * P, :].rearrange(
-                        "q (k c) t -> q k c t", k=2
-                    ),
-                    in_=flipped[:].rearrange("q k t c -> q k c t"),
-                )
+            xt_words = live["xt", u][:].rearrange("q c t -> q (c t)").bitcast(F32)
+            nc.scalar.copy(
+                out=xt_words[:, half * C : (half + 1) * C].rearrange("q (k c h) -> q k c h", k=2, h=2),
+                in_=bank[:].rearrange("q k h c -> q k c h"),
+            )
 
         def quantise_x(u):
             x_codes = stream.tile([P, GROUP], U32, align_bytes=64)
@@ -205,99 +193,90 @@ def tile_efficientmultiscaledilatedattention_pa_t_kernel(tc, x, W_kv, b_kv, E_k,
                 in_=live["kv", u][:, cols, :].rearrange("p c m -> p (c m)"),
             )
 
-        def compress(b):
-            comp = [
-                psum.tile([J, C], F32, name="comp_k", tag="prod_v", bufs=3),
-                psum.tile([J, C], F32, name="comp_v", tag="prod_v", bufs=3),
-            ]
+        def compress(b, s):
+            cols = slice(s * C, (s + 1) * C)
+            comp = psum.tile([J, C], F32, tag="prod_v", bufs=3)
             for g in range(GROUPS):
                 u = b * GROUPS + g
-                for s in range(2):
-                    cols = slice(s * C, (s + 1) * C)
-                    nc.tensor.matmul_mx(
-                        out=comp[s][:],
-                        lhsT=e_codes[:, g, s].bitcast(FP8X4),
-                        lhsT_scale=e_scales[:, g, s],
-                        rhs=live["kv_codes", u][:, cols].bitcast(FP8X4),
-                        rhs_scale=live["kv_scales", u][:, cols],
-                        start=(g == 0),
-                        stop=(g == GROUPS - 1),
-                    )
-            for s, out_dram in enumerate((out_0, out_1)):
-                result = stream.tile([J, C], F32)
-                nc.scalar.copy(out=result[:], in_=comp[s][:])
-                nc.sync.dma_start(
-                    out=out_dram[b].rearrange("h j d -> j h d"),
-                    in_=result[:].rearrange("j (h d) -> j h d", h=HEADS),
+                nc.tensor.matmul_mx(
+                    out=comp[:],
+                    lhsT=e_codes[:, g, s].bitcast(FP8X4),
+                    lhsT_scale=e_scales[:, g, s],
+                    rhs=live["kv_codes", u][:, cols].bitcast(FP8X4),
+                    rhs_scale=live["kv_scales", u][:, cols],
+                    start=(g == 0),
+                    stop=(g == GROUPS - 1),
                 )
+            result = stream.tile([J, C], F32)
+            nc.scalar.copy(out=result[:], in_=comp[:])
+            nc.sync.dma_start(
+                out=(out_0, out_1)[s][b].rearrange("h j d -> j h d"),
+                in_=result[:].rearrange("j (h d) -> j h d", h=HEADS),
+            )
 
         ident = const.tile([P, P], BF16)
         make_identity(nc, ident[:])
         ident_words = const.tile([P, P], F32)
         make_identity(nc, ident_words[:])
-        bias_rows = const.tile([P, KV], BF16)
+        bias_rows = const.tile([P, P], BF16)
         nc.vector.memset(bias_rows[:].bitcast(I32), 0)
-        nc.scalar.dma_start(out=bias_rows[0:1, :], in_=b_kv.rearrange("(o c) -> o c", o=1))
-        ones = const.tile([P, P], BF16)
-        nc.vector.memset(ones[:], 1.0)
+        nc.scalar.dma_start(out=bias_rows[0:SLICES, :], in_=b_kv.rearrange("(s c) -> s c", c=P))
 
+        load(0)
         w_raw = const.tile([P, PACK, KV], BF16)
-        w_rows = W_kv.rearrange("(t q) c -> q t c", t=PACK)
+        w_rows = W_kv.rearrange("(h q e) c -> h q e c", h=2, e=2)
         for half in range(2):
             cols = slice(half * C, (half + 1) * C)
-            nc.sync.dma_start(out=w_raw[:, :, cols], in_=w_rows[:, :, cols])
-        load(0)
-        load(1)
-        load(2)
+            for h in range(2):
+                nc.sync.dma_start(out=w_raw[:, 2 * h : 2 * h + 2, cols], in_=w_rows[h, :, :, cols])
+        for u in range(1, FIRST_LOADS):
+            load(u)
         e_raw = const.tile([P, GROUPS, 2, PACK, J], BF16)
         for g in range(GROUPS):
-            order = "(p m) j -> p m j" if is_tail(g) else "(m p) j -> p m j"
             for s, e_dram in enumerate((E_k, E_v)):
                 nc.sync.dma_start(
                     out=e_raw[:, g, s],
-                    in_=e_dram[g * GROUP : (g + 1) * GROUP, :].rearrange(order, m=PACK),
+                    in_=e_dram[g * GROUP : (g + 1) * GROUP, :].rearrange("(p m) j -> p m j", m=PACK),
                 )
-
-        pair_sum = const.tile([P, P // 2], BF16)
-        ident_pairs = ident[:].rearrange("p (l two) -> p l two", two=2)
-        nc.vector.tensor_tensor(
-            out=pair_sum[:], in0=ident_pairs[:, :, 0], in1=ident_pairs[:, :, 1], op=ADD
-        )
-        bias = const.tile([P, KV], BF16)
-        for half in range(2):
-            cols = slice(half * C, (half + 1) * C)
-            spread = psum.tile([P, C], F32, tag="prod_v", bufs=3)
-            nc.tensor.matmul(
-                out=spread[:], lhsT=ones[:], rhs=bias_rows[:, cols], start=True, stop=True
-            )
-            nc.scalar.copy(out=bias[:, cols], in_=spread[:])
-        upright = psum.tile([P, SLICES], F32, tag="prod_v", bufs=3)
-        for cs in range(SLICES):
-            nc.tensor.matmul(
-                out=upright[:, cs : cs + 1],
-                lhsT=bias_rows[:, cs * P : (cs + 1) * P],
-                rhs=ones[:, 0:1],
-                start=True,
-                stop=True,
-            )
-        bias_cols = const.tile([P, SLICES], F32)
-        nc.scalar.copy(out=bias_cols[:], in_=upright[:])
 
         w_grouped = const.tile([P, KV, PACK], BF16, align_bytes=64)
         w_codes = const.tile([P, KV], U32, align_bytes=64)
         w_scales = const.tile([P, KV], U8, align_bytes=64)
-        for half in range(2):
+
+        def prepare_w(half):
             cols = slice(half * C, (half + 1) * C)
             nc.vector.tensor_copy(
                 out=w_grouped[:, cols, :], in_=w_raw[:, :, cols].rearrange("q t c -> q c t")
             )
-        for half in range(2):
-            cols = slice(half * C, (half + 1) * C)
             nc.vector.quantize_mx(
                 out=w_codes[:, cols].bitcast(FP8X4),
                 scales=w_scales[:, cols],
                 in_=w_grouped[:, cols, :].rearrange("q c t -> q (c t)"),
             )
+
+        bias = const.tile([P, KV], BF16)
+        bias_cols = const.tile([P, SLICES], F32)
+
+        def spread_bias():
+            for half in range(2):
+                spread = psum.tile([P, HALF, P], F32, tag="prod_v", bufs=3)
+                for n in range(HALF):
+                    cs = half * HALF + n
+                    nc.tensor.matmul(
+                        out=spread[:, n, :],
+                        lhsT=ident[:, cs : cs + 1].to_broadcast([P, P]),
+                        rhs=bias_rows[:],
+                        start=True,
+                        stop=True,
+                    )
+                nc.scalar.copy(
+                    out=bias[:, half * C : (half + 1) * C], in_=spread[:].rearrange("p n c -> p (n c)")
+                )
+            upright = psum.tile([P, SLICES], F32, tag="prod_v", bufs=3)
+            nc.tensor.matmul(
+                out=upright[:], lhsT=bias_rows[:], rhs=ident[:, 0:SLICES], start=True, stop=True
+            )
+            nc.scalar.copy(out=bias_cols[:], in_=upright[:])
 
         e_grouped = const.tile([P, GROUPS, 2, J, PACK], BF16, align_bytes=64)
         e_codes = const.tile([P, GROUPS, 2, J], U32, align_bytes=64)
@@ -313,38 +292,50 @@ def tile_efficientmultiscaledilatedattention_pa_t_kernel(tc, x, W_kv, b_kv, E_k,
                 in_=e_grouped[:, g].rearrange("p s j m -> p (s j m)"),
             )
 
-        for i in range(-2, UNITS + 2):
+        for half in range(2):
+            pool(0, half)
+            sums(0, half)
+        spread_bias()
+        prepare_w(0)
+        quantise_x(0)
+        prepare_w(1)
+        pool(1, 0)
+        pool(1, 1)
+        for i in range(-1, UNITS + 1):
             now, before, ahead = is_unit(i), is_unit(i - 1), is_unit(i + 2)
-            if is_unit(i + LOAD_AHEAD) and i + LOAD_AHEAD > 2:
+            if is_unit(i + LOAD_AHEAD):
                 load(i + LOAD_AHEAD)
-            if 0 <= i - 1 < GROUPS:
-                quantise_e(i - 1)
-            if is_unit(i + 1):
-                quantise_x(i + 1)
             if now:
                 new_kv(i)
                 turned(i, 0)
                 direct(i, 2)
+                direct(i, 3)
+            if 0 <= i - 1 < GROUPS:
+                quantise_e(i - 1)
             if before:
                 turn(i - 1, 1)
-            if ahead:
-                sums(i + 2, 0)
-            if now:
-                direct(i, 3)
-                turned(i, 1)
+            if before and is_tail(i - 1):
+                compress((i - 1) // GROUPS, 0)
+            if ahead and i >= 0:
+                pool(i + 2, 0)
+                pool(i + 2, 1)
+            if is_unit(i + 1) and i >= 0:
+                quantise_x(i + 1)
             if before:
                 quantise_kv(i - 1, 1)
             if now:
+                turned(i, 1)
                 turn(i, 0)
             if ahead:
-                sums(i + 2, 1)
+                sums(i + 2, 0)
             if now:
                 direct(i, 6)
                 direct(i, 7)
-                quantise_kv(i, 0)
             if before and is_tail(i - 1):
-                compress((i - 1) // GROUPS)
-            if is_unit(i + 3) and is_tail(i + 3):
-                pool_tail(i + 3)
+                compress((i - 1) // GROUPS, 1)
+            if now:
+                quantise_kv(i, 0)
+            if ahead:
+                sums(i + 2, 1)
             if 0 <= i < GROUPS:
                 regroup_e(i)

from contextlib import ExitStack

import concourse.mybir as mybir
from concourse.masks import make_identity

BF16 = mybir.dt.bfloat16
F32 = mybir.dt.float32
I32 = mybir.dt.int32
U32 = mybir.dt.uint32
U8 = mybir.dt.uint8
FP8X4 = mybir.dt.float8_e4m3fn_x4
ADD = mybir.AluOpType.add
MULT = mybir.AluOpType.mult
IDENTITY = mybir.ActivationFunctionType.Identity

P = 128
PACK = 4
B = 4
C = 512
KV = 2 * C
SLICES = KV // P
J = 128
HEADS = 4
GROUPS = 3
UNITS = B * GROUPS
GROUP = P * PACK
TOKENS = 2 * GROUP
SLOTS = TOKENS // P
LOAD_AHEAD = 5
FIRST_LOADS = 4
HALF = SLICES // 2
TURNED = 2

FLOPS = 2 * B * GROUPS * GROUP * C * KV + 2 * B * 2 * J * GROUPS * GROUP * C


def load_dense_tokens(nc, x_group, xg):
    rows = x_group.rearrange("(p i) c -> p i c", i=SLOTS)
    for half in range(2):
        part = slice(half * SLOTS // 2, (half + 1) * SLOTS // 2)
        nc.sync.dma_start(out=xg[:, part, :], in_=rows[:, part, :])


def load_tail_tokens(nc, x_b, xg):
    nc.sync.dma_start(out=xg[0:32], in_=x_b[2048:2304, :].rearrange("(p i) c -> p i c", i=SLOTS))
    step2 = x_b.rearrange("(r rr w i ii) c -> rr w ii r i c", rr=2, w=3, i=SLOTS, ii=2)
    for w in range(3):
        nc.sync.dma_start(out=xg[32 + w : 104 : 3], in_=step2[0, w, 0])
    step3 = x_b.rearrange("(r rr w i ii) c -> rr w ii r i c", rr=3, w=2, i=SLOTS, ii=3)
    for w in range(2):
        nc.sync.dma_start(out=xg[104 + w : 128 : 2], in_=step3[0, w, 0, 0:12])


def tile_efficientmultiscaledilatedattention_pa_t_kernel(tc, x, W_kv, b_kv, E_k, E_v, out_0, out_1):
    nc = tc.nc
    with ExitStack() as ctx:
        const = ctx.enter_context(tc.tile_pool(name="const", bufs=1))
        stream = ctx.enter_context(tc.tile_pool(name="stream", bufs=2))
        psum = ctx.enter_context(tc.psum_pool(name="psum", bufs=1))
        ctx.enter_context(tc.manual_schedule())

        live = {}

        def is_unit(u):
            return 0 <= u < UNITS

        def is_tail(u):
            return u % GROUPS == GROUPS - 1

        def load(u):
            b, g = divmod(u, GROUPS)
            xg = stream.tile([P, SLOTS, C], BF16, bufs=4)
            if is_tail(u):
                load_tail_tokens(nc, x[b], xg)
            else:
                load_dense_tokens(nc, x[b, g * TOKENS : (g + 1) * TOKENS, :], xg)
            live["xg", u] = xg

        def pool(u, half):
            if half == 0:
                live["xs", u] = stream.tile([P, PACK, C], BF16, name="xs")
            pairs = live["xg", u][:].rearrange("p (m two) c -> p m two c", two=2)
            two_m = slice(2 * half, 2 * half + 2)
            nc.vector.tensor_tensor(
                out=live["xs", u][:, two_m, :],
                in0=pairs[:, two_m, 0, :],
                in1=pairs[:, two_m, 1, :],
                op=ADD,
            )

        def sums(u, half):
            if half == 0:
                live["xt", u] = stream.tile([P, GROUP, PACK], BF16, name="xt", align_bytes=64)
            bank = psum.tile([P, 2, 2, P], F32, tag="xl", bufs=2)
            words = live["xs", u][:].rearrange("p m c -> p (m c)").bitcast(F32)
            for k in range(2):
                for h in range(2):
                    start = ((2 * half + k) * 2 + h) * P
                    nc.tensor.transpose(
                        out=bank[:, k, h, :], in_=words[:, start : start + P], identity=ident_words[:]
                    )
            xt_words = live["xt", u][:].rearrange("q c t -> q (c t)").bitcast(F32)
            nc.scalar.copy(
                out=xt_words[:, half * C : (half + 1) * C].rearrange("q (k c h) -> q k c h", k=2, h=2),
                in_=bank[:].rearrange("q k h c -> q k c h"),
            )

        def quantise_x(u):
            x_codes = stream.tile([P, GROUP], U32, align_bytes=64)
            x_scales = stream.tile([P, GROUP], U8, align_bytes=64)
            nc.vector.quantize_mx(
                out=x_codes[:].bitcast(FP8X4),
                scales=x_scales[:],
                in_=live["xt", u][:].rearrange("q c t -> q (c t)"),
            )
            live["x_codes", u] = x_codes
            live["x_scales", u] = x_scales

        def new_kv(u):
            live["kv", u] = stream.tile([P, KV, PACK], BF16, name="kv", align_bytes=64)

        def direct(u, cs):
            x_codes, x_scales = live["x_codes", u], live["x_scales", u]
            cols = slice(cs * P, (cs + 1) * P)
            prod = psum.tile([P, PACK, P], F32, tag="prod_v", bufs=3)
            for m in range(PACK):
                nc.tensor.matmul_mx(
                    out=prod[:, m, :],
                    lhsT=x_codes[:, m * P : (m + 1) * P].bitcast(FP8X4),
                    lhsT_scale=x_scales[:, m * P : (m + 1) * P],
                    rhs=w_codes[:, cols].bitcast(FP8X4),
                    rhs_scale=w_scales[:, cols],
                    start=True,
                    stop=True,
                )
            nc.vector.scalar_tensor_tensor(
                out=live["kv", u][:, cols, :],
                in0=prod[:].rearrange("p m c -> p c m"),
                scalar=0.5,
                in1=bias[:, cols].unsqueeze(2).to_broadcast([P, P, PACK]),
                op0=MULT,
                op1=ADD,
            )

        def turned(u, half):
            x_codes, x_scales = live["x_codes", u], live["x_scales", u]
            flat = stream.tile([P, TURNED, 2, P, 2], BF16, name="flat", align_bytes=64, bufs=3)
            for n in range(TURNED):
                cs = half * HALF + n
                cols = slice(cs * P, (cs + 1) * P)
                prod = psum.tile([P, GROUP], F32, tag="prod_s", bufs=2)
                nc.tensor.matmul_mx(
                    out=prod[:],
                    lhsT=w_codes[:, cols].bitcast(FP8X4),
                    lhsT_scale=w_scales[:, cols],
                    rhs=x_codes[:].bitcast(FP8X4),
                    rhs_scale=x_scales[:],
                    start=True,
                    stop=True,
                )
                nc.scalar.activation(
                    out=flat[:, n],
                    in_=prod[:].rearrange("c (h e p) -> c h p e", h=2, e=2),
                    func=IDENTITY,
                    bias=bias_cols[:, cs : cs + 1],
                    scale=0.5,
                )
            live["flat", u, half] = flat

        def turn(u, half):
            words = live["flat", u, half][:].rearrange("c n h p e -> c (n h) (p e)").bitcast(F32)
            bank = psum.tile([P, TURNED, 2, P], F32, tag="turned", bufs=1)
            for n in range(TURNED):
                for h in range(2):
                    nc.tensor.transpose(
                        out=bank[:, n, h, :], in_=words[:, 2 * n + h, :], identity=ident_words[:]
                    )
            cols = slice(half * C, half * C + TURNED * P)
            kv_words = live["kv", u][:, cols, :].rearrange("p c m -> p (c m)").bitcast(F32)
            nc.scalar.copy(
                out=kv_words.rearrange("p (n c h) -> p n c h", n=TURNED, h=2),
                in_=bank[:].rearrange("p n h c -> p n c h"),
            )

        def quantise_kv(u, half):
            if half == 0:
                live["kv_codes", u] = stream.tile([P, KV], U32, name="kv_codes", bufs=4, align_bytes=64)
                live["kv_scales", u] = stream.tile([P, KV], U8, name="kv_scales", bufs=4, align_bytes=64)
            cols = slice(half * C, (half + 1) * C)
            nc.vector.quantize_mx(
                out=live["kv_codes", u][:, cols].bitcast(FP8X4),
                scales=live["kv_scales", u][:, cols],
                in_=live["kv", u][:, cols, :].rearrange("p c m -> p (c m)"),
            )

        def compress(b, s):
            cols = slice(s * C, (s + 1) * C)
            comp = psum.tile([J, C], F32, tag="prod_v", bufs=3)
            for g in range(GROUPS):
                u = b * GROUPS + g
                nc.tensor.matmul_mx(
                    out=comp[:],
                    lhsT=e_codes[:, g, s].bitcast(FP8X4),
                    lhsT_scale=e_scales[:, g, s],
                    rhs=live["kv_codes", u][:, cols].bitcast(FP8X4),
                    rhs_scale=live["kv_scales", u][:, cols],
                    start=(g == 0),
                    stop=(g == GROUPS - 1),
                )
            result = stream.tile([J, C], F32)
            nc.scalar.copy(out=result[:], in_=comp[:])
            nc.sync.dma_start(
                out=(out_0, out_1)[s][b].rearrange("h j d -> j h d"),
                in_=result[:].rearrange("j (h d) -> j h d", h=HEADS),
            )

        ident = const.tile([P, P], BF16)
        make_identity(nc, ident[:])
        ident_words = const.tile([P, P], F32)
        make_identity(nc, ident_words[:])
        bias_rows = const.tile([P, P], BF16)
        nc.vector.memset(bias_rows[:].bitcast(I32), 0)
        nc.scalar.dma_start(out=bias_rows[0:SLICES, :], in_=b_kv.rearrange("(s c) -> s c", c=P))

        load(0)
        w_raw = const.tile([P, PACK, KV], BF16)
        w_rows = W_kv.rearrange("(h q e) c -> h q e c", h=2, e=2)
        for half in range(2):
            cols = slice(half * C, (half + 1) * C)
            for h in range(2):
                nc.sync.dma_start(out=w_raw[:, 2 * h : 2 * h + 2, cols], in_=w_rows[h, :, :, cols])
        for u in range(1, FIRST_LOADS):
            load(u)
        e_raw = const.tile([P, GROUPS, 2, PACK, J], BF16)
        for g in range(GROUPS):
            for s, e_dram in enumerate((E_k, E_v)):
                nc.sync.dma_start(
                    out=e_raw[:, g, s],
                    in_=e_dram[g * GROUP : (g + 1) * GROUP, :].rearrange("(p m) j -> p m j", m=PACK),
                )

        w_grouped = const.tile([P, KV, PACK], BF16, align_bytes=64)
        w_codes = const.tile([P, KV], U32, align_bytes=64)
        w_scales = const.tile([P, KV], U8, align_bytes=64)

        def prepare_w(half):
            cols = slice(half * C, (half + 1) * C)
            nc.vector.tensor_copy(
                out=w_grouped[:, cols, :], in_=w_raw[:, :, cols].rearrange("q t c -> q c t")
            )
            nc.vector.quantize_mx(
                out=w_codes[:, cols].bitcast(FP8X4),
                scales=w_scales[:, cols],
                in_=w_grouped[:, cols, :].rearrange("q c t -> q (c t)"),
            )

        bias = const.tile([P, KV], BF16)
        bias_cols = const.tile([P, SLICES], F32)

        def spread_bias():
            for half in range(2):
                spread = psum.tile([P, HALF, P], F32, tag="prod_v", bufs=3)
                for n in range(HALF):
                    cs = half * HALF + n
                    nc.tensor.matmul(
                        out=spread[:, n, :],
                        lhsT=ident[:, cs : cs + 1].to_broadcast([P, P]),
                        rhs=bias_rows[:],
                        start=True,
                        stop=True,
                    )
                nc.scalar.copy(
                    out=bias[:, half * C : (half + 1) * C], in_=spread[:].rearrange("p n c -> p (n c)")
                )
            upright = psum.tile([P, SLICES], F32, tag="prod_v", bufs=3)
            nc.tensor.matmul(
                out=upright[:], lhsT=bias_rows[:], rhs=ident[:, 0:SLICES], start=True, stop=True
            )
            nc.scalar.copy(out=bias_cols[:], in_=upright[:])

        e_grouped = const.tile([P, GROUPS, 2, J, PACK], BF16, align_bytes=64)
        e_codes = const.tile([P, GROUPS, 2, J], U32, align_bytes=64)
        e_scales = const.tile([P, GROUPS, 2, J], U8, align_bytes=64)

        def regroup_e(g):
            nc.scalar.copy(out=e_grouped[:, g], in_=e_raw[:, g].rearrange("p s m j -> p s j m"))

        def quantise_e(g):
            nc.vector.quantize_mx(
                out=e_codes[:, g].rearrange("p s j -> p (s j)").bitcast(FP8X4),
                scales=e_scales[:, g].rearrange("p s j -> p (s j)"),
                in_=e_grouped[:, g].rearrange("p s j m -> p (s j m)"),
            )

        for half in range(2):
            pool(0, half)
            sums(0, half)
        spread_bias()
        prepare_w(0)
        quantise_x(0)
        prepare_w(1)
        pool(1, 0)
        pool(1, 1)
        for i in range(-1, UNITS + 1):
            now, before, ahead = is_unit(i), is_unit(i - 1), is_unit(i + 2)
            if is_unit(i + LOAD_AHEAD):
                load(i + LOAD_AHEAD)
            if now:
                new_kv(i)
                turned(i, 0)
                direct(i, 2)
                direct(i, 3)
            if 0 <= i - 1 < GROUPS:
                quantise_e(i - 1)
            if before:
                turn(i - 1, 1)
            if before and is_tail(i - 1):
                compress((i - 1) // GROUPS, 0)
            if ahead and i >= 0:
                pool(i + 2, 0)
                pool(i + 2, 1)
            if is_unit(i + 1) and i >= 0:
                quantise_x(i + 1)
            if before:
                quantise_kv(i - 1, 1)
            if now:
                turned(i, 1)
                turn(i, 0)
            if ahead:
                sums(i + 2, 0)
            if now:
                direct(i, 6)
                direct(i, 7)
            if before and is_tail(i - 1):
                compress((i - 1) // GROUPS, 1)
            if now:
                quantise_kv(i, 0)
            if ahead:
                sums(i + 2, 1)
            if 0 <= i < GROUPS:
                regroup_e(i)
